import numpy as np
import ml_dtypes


def mxq(x, axis, fmt="e4m3"):
    dtype, down = {"e4m3": (ml_dtypes.float8_e4m3fn, 7), "e5m2": (ml_dtypes.float8_e5m2, 14)}[fmt]
    v = np.moveaxis(np.asarray(x, np.float32).astype(ml_dtypes.bfloat16).astype(np.float64), axis, -1)
    blocks = v.reshape(v.shape[:-1] + (-1, 32))
    amax = np.abs(blocks).max(-1, keepdims=True)
    byte = np.maximum(np.where(amax > 0, np.frexp(amax)[1] - 1 + 127, 0) - down, 1)
    scale = np.exp2(byte - 127.0)
    codes = (blocks / scale).astype(np.float32).astype(dtype).astype(np.float64)
    return np.moveaxis((codes * scale).reshape(v.shape), -1, axis)


WIDE = False


def mx_kscale(k):
    if not WIDE:
        return np.ones(k)
    levels = np.array([10, -10, 5, -5, 0])
    a = np.random.permutation(np.resize(levels, k // 512 * 4)).reshape(k // 512, 4)
    idx = np.arange(k)
    return np.exp2(a[idx // 512, idx % 128 // 32])


BF16 = ml_dtypes.bfloat16


def bf(x):
    return np.asarray(x, np.float32).astype(BF16)


def f64(x):
    return np.asarray(x).astype(np.float64)


B, C, HID, HS = 4, 2048, 1024, 16
HH = HID // 2
CIN2 = HID + HH
P = HS * HS


def setup_inputs():
    s, t = mx_kscale(C), mx_kscale(HID)
    u = np.concatenate([t, t[HH:]])
    return {"x": bf(np.random.standard_normal((B, C, HS, HS)) * s[None, :, None, None]),
            "w1": bf(np.random.standard_normal((C, HID)) / np.sqrt(C) / s[:, None] * t),
            "b1": bf(np.random.standard_normal(HID) * 0.2 * t),
            "w2": bf(np.random.standard_normal((CIN2, C)) / np.sqrt(CIN2) / u[:, None]),
            "b2": bf(np.random.standard_normal(C) * 0.2)}


def reference(x, w1, b1, w2, b2):
    xq = mxq(f64(x).reshape(B, C, P), 1, "e4m3")
    y = (mxq(f64(w1), 0, "e4m3").T @ xq) + f64(b1)[None, :, None]
    a, fmap = np.split(y, 2, axis=1)
    z = np.concatenate([a, fmap, np.maximum(fmap, 0.0)], axis=1)
    o = (mxq(f64(w2), 0, "e4m3").T @ mxq(z, 1, "e4m3")) + f64(b2)[None, :, None]
    return o.reshape(B, C, HS, HS)

@@ -1,0 +1,241 @@
+from contextlib import ExitStack
+
+import concourse.mybir as mybir
+from concourse.masks import make_identity
+
+F32 = mybir.dt.float32
+BF16 = mybir.dt.bfloat16
+U32 = mybir.dt.uint32
+U8 = mybir.dt.uint8
+FP8X4 = mybir.dt.float8_e4m3fn_x4
+IDENTITY = mybir.ActivationFunctionType.Identity
+
+P = 128
+PACK = 4
+K_PASS = P * PACK
+
+IMAGES, C_IN, HIDDEN, PIXELS = 4, 2048, 1024, 256
+C_MID = HIDDEN + HIDDEN // 2
+C_OUT = 2048
+COLS = IMAGES * PIXELS
+N_TILE = 512
+HALVES = COLS // N_TILE
+PASSES_1 = C_IN // K_PASS
+PASSES_2 = C_MID // K_PASS
+M_TILES_1 = HIDDEN // P
+M_TILES_2 = C_OUT // P
+BLOCK = 512
+W2_BLOCKS = C_OUT // BLOCK
+RUN = 4
+PLAIN, RECTIFIED = 0, 1
+
+FLOPS = 2 * COLS * (C_IN * HIDDEN + C_MID * C_OUT)
+
+
+def tile_offm_pa_kernel(tc, x, w1, b1, w2, b2, out):
+    nc = tc.nc
+    with ExitStack() as ctx:
+        ctx.enter_context(tc.manual_schedule())
+        keep = ctx.enter_context(tc.tile_pool(name="keep", bufs=1))
+        grouped_pool = ctx.enter_context(tc.tile_pool(name="grouped", bufs=8))
+        y_pool = ctx.enter_context(tc.tile_pool(name="y", bufs=2))
+        o_pool = ctx.enter_context(tc.tile_pool(name="o", bufs=6))
+        psum = ctx.enter_context(tc.psum_pool(name="psum", bufs=8))
+
+        w1_codes = keep.tile([P, PASSES_1, HIDDEN], U32, align_bytes=64)
+        w1_scales = keep.tile([P, PASSES_1, HIDDEN], U8, align_bytes=64)
+        x_codes = keep.tile([P, PASSES_1, COLS], U32, align_bytes=64)
+        x_scales = keep.tile([P, PASSES_1, COLS], U8, align_bytes=64)
+        z_codes = keep.tile([P, PASSES_2, COLS], U32, align_bytes=64)
+        z_scales = keep.tile([P, PASSES_2, COLS], U8, align_bytes=64)
+        w2_codes = keep.tile([P, PASSES_2, C_OUT], U32, align_bytes=64)
+        w2_scales = keep.tile([P, PASSES_2, C_OUT], U8, align_bytes=64)
+
+        def regroup_views(grouped_cols, rows):
+            return (
+                grouped_cols.rearrange("p (c i) t -> p c t i", i=RUN),
+                rows.rearrange("p t (c i) -> p c t i", i=RUN),
+            )
+
+        def regroup_on_vector(grouped_cols, rows):
+            dst, src = regroup_views(grouped_cols, rows)
+            nc.vector.tensor_copy(out=dst, in_=src)
+
+        def regroup_on_scalar(grouped_cols, rows):
+            dst, src = regroup_views(grouped_cols, rows)
+            nc.scalar.copy(out=dst, in_=src)
+
+        def new_grouped():
+            return grouped_pool.tile([P, BLOCK, PACK], BF16, align_bytes=64, name="grouped", tag="grouped")
+
+        def quantise(grouped, codes, scales):
+            nc.vector.quantize_mx(
+                out=codes.bitcast(FP8X4), scales=scales, in_=grouped[:].rearrange("p w t -> p (w t)")
+            )
+
+        def new_bank():
+            return psum.tile([P, N_TILE], F32, name="acc", tag="acc")
+
+        def first_contraction_pass(acc, g, m, half):
+            nc.tensor.matmul_mx(
+                out=acc[:],
+                lhsT=w1_codes[:, g, m * P : (m + 1) * P].bitcast(FP8X4),
+                lhsT_scale=w1_scales[:, g, m * P : (m + 1) * P],
+                rhs=x_codes[:, g, half * N_TILE : (half + 1) * N_TILE].bitcast(FP8X4),
+                rhs_scale=x_scales[:, g, half * N_TILE : (half + 1) * N_TILE],
+                start=(g == 0),
+                stop=(g == PASSES_1 - 1),
+            )
+
+        def empty_banks(accs, group):
+            y_sb = y_pool.tile([P, PACK, N_TILE], BF16, name="y_sb", tag="y_sb")
+            for t in range(PACK):
+                m = group * PACK + t
+                nc.scalar.activation(
+                    out=y_sb[:, t, :], in_=accs[t][:], func=IDENTITY, bias=bias[:, m : m + 1], scale=1.0
+                )
+            return y_sb
+
+        def quantise_z(y_rect, y_plain, half):
+            cols = slice(half * N_TILE, (half + 1) * N_TILE)
+            z_rect_in = new_grouped()
+            regroup_on_vector(z_rect_in[:], y_rect[:])
+            z_plain = new_grouped()
+            regroup_on_vector(z_plain[:], y_plain[:])
+            z_rect_out = new_grouped()
+            nc.vector.tensor_scalar_max(out=z_rect_out[:], in0=z_rect_in[:], scalar1=0.0)
+            quantise(z_rect_in, z_codes[:, 1, cols], z_scales[:, 1, cols])
+            quantise(z_plain, z_codes[:, 0, cols], z_scales[:, 0, cols])
+            quantise(z_rect_out, z_codes[:, 2, cols], z_scales[:, 2, cols])
+
+        with tc.tile_pool(name="raw1", bufs=1) as raw1:
+            ident = keep.tile([P, P], BF16)
+            make_identity(nc, ident[:])
+            bias_rows = keep.tile([P, P], BF16)
+            nc.vector.memset(bias_rows[:], 0.0)
+            nc.sync.dma_start(out=bias_rows[0:M_TILES_1, :], in_=b1.rearrange("(m p) -> m p", p=P))
+            nc.sync.dma_start(
+                out=bias_rows[M_TILES_1 : M_TILES_1 + M_TILES_2, :], in_=b2.rearrange("(m p) -> m p", p=P)
+            )
+            bias_ps = psum.tile([P, P], BF16, tag="acc")
+            nc.tensor.transpose(bias_ps[:], bias_rows[:], ident[:])
+            bias = keep.tile([P, M_TILES_1 + M_TILES_2], F32)
+            nc.vector.tensor_copy(out=bias[:], in_=bias_ps[:, 0 : M_TILES_1 + M_TILES_2])
+
+            w1_raw = []
+            x_raw = [[], []]
+            for half in range(HALVES):
+                for g in range(PASSES_1):
+                    k_rows = slice(g * K_PASS, (g + 1) * K_PASS)
+                    if half == 0:
+                        w_rows = raw1.tile([P, PACK, HIDDEN], BF16, name="w1_raw%d" % g)
+                        nc.sync.dma_start(out=w_rows[:], in_=w1[k_rows, :].rearrange("(p j) d -> p j d", j=PACK))
+                        w1_raw.append(w_rows)
+                    x_rows = raw1.tile([P, 2, PACK, PIXELS], BF16, name="x_raw%d_%d" % (half, g))
+                    nc.sync.dma_start(
+                        out=x_rows[:],
+                        in_=x[2 * half : 2 * half + 2, k_rows].rearrange("b (p j) r c -> p b j (r c)", j=PACK),
+                    )
+                    x_raw[half].append(x_rows)
+
+            def regroup_images(x_rows, scalar_helps):
+                grouped = new_grouped()
+                regroup_on_vector(grouped[:, 0:PIXELS, :], x_rows[:, 0])
+                if scalar_helps:
+                    regroup_on_scalar(grouped[:, PIXELS : 2 * PIXELS, :], x_rows[:, 1])
+                else:
+                    regroup_on_vector(grouped[:, PIXELS : 2 * PIXELS, :], x_rows[:, 1])
+                return grouped
+
+            first_accs = {}
+            for group in (RECTIFIED, PLAIN):
+                first_accs[group] = [new_bank() for t in range(PACK)]
+            for g in range(PASSES_1):
+                w_left = new_grouped()
+                regroup_on_vector(w_left[:], w1_raw[g][:, :, 0:BLOCK])
+                w_right = new_grouped()
+                regroup_on_scalar(w_right[:], w1_raw[g][:, :, BLOCK : 2 * BLOCK])
+                x_grouped = regroup_images(x_raw[0][g], True)
+                quantise(w_left, w1_codes[:, g, 0:BLOCK], w1_scales[:, g, 0:BLOCK])
+                quantise(w_right, w1_codes[:, g, BLOCK : 2 * BLOCK], w1_scales[:, g, BLOCK : 2 * BLOCK])
+                quantise(x_grouped, x_codes[:, g, 0:N_TILE], x_scales[:, g, 0:N_TILE])
+                for group in (RECTIFIED, PLAIN):
+                    for t in range(PACK):
+                        first_contraction_pass(first_accs[group][t], g, group * PACK + t, 0)
+
+            for first_g in range(0, PASSES_1, 2):
+                pair = [regroup_images(x_raw[1][g], first_g == 0) for g in (first_g, first_g + 1)]
+                for g, x_grouped in zip((first_g, first_g + 1), pair):
+                    quantise(x_grouped, x_codes[:, g, N_TILE:COLS], x_scales[:, g, N_TILE:COLS])
+                if first_g == 0:
+                    y_rect = empty_banks(first_accs[RECTIFIED], RECTIFIED)
+                    y_plain = empty_banks(first_accs[PLAIN], PLAIN)
+
+        with tc.tile_pool(name="raw2", bufs=1, reuse_waits="tile") as raw2:
+            w2_raw = []
+            for c in range(W2_BLOCKS):
+                for g in range(PASSES_2):
+                    w_rows = raw2.tile([P, PACK, BLOCK], BF16, name="w2_raw%d_%d" % (c, g))
+                    nc.sync.dma_start(
+                        out=w_rows[:],
+                        in_=w2[g * K_PASS : (g + 1) * K_PASS, c * BLOCK : (c + 1) * BLOCK].rearrange(
+                            "(t p) e -> p t e", p=P
+                        ),
+                    )
+                    w2_raw.append(w_rows)
+
+            def quantise_w2(c):
+                cols = slice(c * BLOCK, (c + 1) * BLOCK)
+                grouped = []
+                for g in range(PASSES_2):
+                    w_rows = w2_raw[c * PASSES_2 + g]
+                    w_grouped = new_grouped()
+                    regroup_on_vector(w_grouped[:, 0 : BLOCK // 2, :], w_rows[:, :, 0 : BLOCK // 2])
+                    regroup_on_scalar(w_grouped[:, BLOCK // 2 : BLOCK, :], w_rows[:, :, BLOCK // 2 : BLOCK])
+                    grouped.append(w_grouped)
+                for g in range(PASSES_2):
+                    quantise(grouped[g], w2_codes[:, g, cols], w2_scales[:, g, cols])
+
+            def second_contraction(c):
+                for half in range(HALVES):
+                    n_cols = slice(half * N_TILE, (half + 1) * N_TILE)
+                    for m in range(c * BLOCK // P, (c + 1) * BLOCK // P):
+                        acc = new_bank()
+                        for g in range(PASSES_2):
+                            nc.tensor.matmul_mx(
+                                out=acc[:],
+                                lhsT=w2_codes[:, g, m * P : (m + 1) * P].bitcast(FP8X4),
+                                lhsT_scale=w2_scales[:, g, m * P : (m + 1) * P],
+                                rhs=z_codes[:, g, n_cols].bitcast(FP8X4),
+                                rhs_scale=z_scales[:, g, n_cols],
+                                start=(g == 0),
+                                stop=(g == PASSES_2 - 1),
+                            )
+                        o_sb = o_pool.tile([P, N_TILE], F32, name="o_sb", tag="o_sb")
+                        b2_col = bias[:, M_TILES_1 + m : M_TILES_1 + m + 1]
+                        if m % 2 == 0:
+                            nc.scalar.activation(out=o_sb[:], in_=acc[:], func=IDENTITY, bias=b2_col, scale=1.0)
+                        else:
+                            nc.vector.tensor_scalar_add(out=o_sb[:], in0=acc[:], scalar1=b2_col)
+                        nc.sync.dma_start(
+                            out=out[2 * half : 2 * half + 2, m * P : (m + 1) * P].rearrange("b e r c -> e b (r c)"),
+                            in_=o_sb[:].rearrange("p (b w) -> p b w", b=2),
+                        )
+
+            second_accs = {}
+            for group in (RECTIFIED, PLAIN):
+                second_accs[group] = [new_bank() for t in range(PACK)]
+                for g in range(PASSES_1):
+                    for t in range(PACK):
+                        first_contraction_pass(second_accs[group][t], g, group * PACK + t, 1)
+
+            quantise_z(y_rect, y_plain, 0)
+            quantise_w2(0)
+            y_rect = empty_banks(second_accs[RECTIFIED], RECTIFIED)
+            y_plain = empty_banks(second_accs[PLAIN], PLAIN)
+            quantise_z(y_rect, y_plain, 1)
+
+            for c in range(W2_BLOCKS):
+                if c + 1 < W2_BLOCKS:
+                    quantise_w2(c + 1)
+                second_contraction(c)

@@ -35,7 +35,6 @@ FLOPS = 2 * COLS * (C_IN * HIDDEN + C_MID * C_OUT)
 def tile_offm_pa_kernel(tc, x, w1, b1, w2, b2, out):
     nc = tc.nc
     with ExitStack() as ctx:
-        ctx.enter_context(tc.manual_schedule())
         keep = ctx.enter_context(tc.tile_pool(name="keep", bufs=1))
         grouped_pool = ctx.enter_context(tc.tile_pool(name="grouped", bufs=8))
         y_pool = ctx.enter_context(tc.tile_pool(name="y", bufs=2))

@@ -26,6 +26,7 @@ M_TILES_1 = HIDDEN // P
 M_TILES_2 = C_OUT // P
 BLOCK = 512
 W2_BLOCKS = C_OUT // BLOCK
+W2_VECTOR_COLS = 320
 RUN = 4
 PLAIN, RECTIFIED = 0, 1
 
@@ -35,6 +36,7 @@ FLOPS = 2 * COLS * (C_IN * HIDDEN + C_MID * C_OUT)
 def tile_offm_pa_kernel(tc, x, w1, b1, w2, b2, out):
     nc = tc.nc
     with ExitStack() as ctx:
+        ctx.enter_context(tc.manual_schedule())
         keep = ctx.enter_context(tc.tile_pool(name="keep", bufs=1))
         grouped_pool = ctx.enter_context(tc.tile_pool(name="grouped", bufs=8))
         y_pool = ctx.enter_context(tc.tile_pool(name="y", bufs=2))
@@ -97,15 +99,15 @@ def tile_offm_pa_kernel(tc, x, w1, b1, w2, b2, out):
 
         def quantise_z(y_rect, y_plain, half):
             cols = slice(half * N_TILE, (half + 1) * N_TILE)
+            z_plain = new_grouped()
+            regroup_on_scalar(z_plain[:], y_plain[:])
             z_rect_in = new_grouped()
             regroup_on_vector(z_rect_in[:], y_rect[:])
-            z_plain = new_grouped()
-            regroup_on_vector(z_plain[:], y_plain[:])
             z_rect_out = new_grouped()
             nc.vector.tensor_scalar_max(out=z_rect_out[:], in0=z_rect_in[:], scalar1=0.0)
             quantise(z_rect_in, z_codes[:, 1, cols], z_scales[:, 1, cols])
-            quantise(z_plain, z_codes[:, 0, cols], z_scales[:, 0, cols])
             quantise(z_rect_out, z_codes[:, 2, cols], z_scales[:, 2, cols])
+            quantise(z_plain, z_codes[:, 0, cols], z_scales[:, 0, cols])
 
         with tc.tile_pool(name="raw1", bufs=1) as raw1:
             ident = keep.tile([P, P], BF16)
@@ -189,8 +191,8 @@ def tile_offm_pa_kernel(tc, x, w1, b1, w2, b2, out):
                 for g in range(PASSES_2):
                     w_rows = w2_raw[c * PASSES_2 + g]
                     w_grouped = new_grouped()
-                    regroup_on_vector(w_grouped[:, 0 : BLOCK // 2, :], w_rows[:, :, 0 : BLOCK // 2])
-                    regroup_on_scalar(w_grouped[:, BLOCK // 2 : BLOCK, :], w_rows[:, :, BLOCK // 2 : BLOCK])
+                    regroup_on_vector(w_grouped[:, 0:W2_VECTOR_COLS, :], w_rows[:, :, 0:W2_VECTOR_COLS])
+                    regroup_on_scalar(w_grouped[:, W2_VECTOR_COLS:BLOCK, :], w_rows[:, :, W2_VECTOR_COLS:BLOCK])
                     grouped.append(w_grouped)
                 for g in range(PASSES_2):
                     quantise(grouped[g], w2_codes[:, g, cols], w2_scales[:, g, cols])
@@ -212,7 +214,7 @@ def tile_offm_pa_kernel(tc, x, w1, b1, w2, b2, out):
                             )
                         o_sb = o_pool.tile([P, N_TILE], F32, name="o_sb", tag="o_sb")
                         b2_col = bias[:, M_TILES_1 + m : M_TILES_1 + m + 1]
-                        if m % 2 == 0:
+                        if m % PACK != PACK - 1:
                             nc.scalar.activation(out=o_sb[:], in_=acc[:], func=IDENTITY, bias=b2_col, scale=1.0)
                         else:
                             nc.vector.tensor_scalar_add(out=o_sb[:], in0=acc[:], scalar1=b2_col)

@@ -27,7 +27,7 @@ M_TILES_2 = C_OUT // P
 BLOCK = 512
 W2_BLOCKS = C_OUT // BLOCK
 W2_VECTOR_COLS = 320
-RUN = 4
+RUN = 8
 PLAIN, RECTIFIED = 0, 1
 
 FLOPS = 2 * COLS * (C_IN * HIDDEN + C_MID * C_OUT)

@@ -27,6 +27,18 @@ M_TILES_2 = C_OUT // P
 BLOCK = 512
 W2_BLOCKS = C_OUT // BLOCK
 W2_VECTOR_COLS = 320
+RECT_V = 512
+LAST_V = 192
+X1_V = (256, 256, 512, 384)
+EV = (0, 0, 0, 1)
+ZP_V = (0, 0)
+W2A_V = 320
+W20 = 512
+EARLY = 0
+LAG = 2
+LAG3 = 2
+W2_V = (320, 320, 384)
+SCHED = ({0: (0, 2, 1, 4, 3, 5)}, {0: (0,), 1: (2, 1), 2: (4, 3), 3: (5,)}, {0: (0,), 1: (2, 1), 2: (4, 3), 3: (5,)})
 RUN = 8
 PLAIN, RECTIFIED = 0, 1
 
@@ -66,12 +78,24 @@ def tile_offm_pa_kernel(tc, x, w1, b1, w2, b2, out):
             dst, src = regroup_views(grouped_cols, rows)
             nc.scalar.copy(out=dst, in_=src)
 
+        def regroup(rows, vector_cols):
+            width = rows.shape[2]
+            grouped = new_grouped()
+            if vector_cols > 0:
+                regroup_on_vector(grouped[:, 0:vector_cols, :], rows[:, :, 0:vector_cols])
+            if vector_cols < width:
+                regroup_on_scalar(grouped[:, vector_cols:width, :], rows[:, :, vector_cols:width])
+            return grouped
+
         def new_grouped():
             return grouped_pool.tile([P, BLOCK, PACK], BF16, align_bytes=64, name="grouped", tag="grouped")
 
         def quantise(grouped, codes, scales):
+            width = codes.shape[1]
             nc.vector.quantize_mx(
-                out=codes.bitcast(FP8X4), scales=scales, in_=grouped[:].rearrange("p w t -> p (w t)")
+                out=codes.bitcast(FP8X4),
+                scales=scales,
+                in_=grouped[:, 0:width, :].rearrange("p w t -> p (w t)"),
             )
 
         def new_bank():
@@ -88,89 +112,115 @@ def tile_offm_pa_kernel(tc, x, w1, b1, w2, b2, out):
                 stop=(g == PASSES_1 - 1),
             )
 
-        def empty_banks(accs, group):
+        def empty_banks(accs, group, by_vector):
             y_sb = y_pool.tile([P, PACK, N_TILE], BF16, name="y_sb", tag="y_sb")
             for t in range(PACK):
-                m = group * PACK + t
-                nc.scalar.activation(
-                    out=y_sb[:, t, :], in_=accs[t][:], func=IDENTITY, bias=bias[:, m : m + 1], scale=1.0
-                )
+                b1_col = bias[:, group * PACK + t : group * PACK + t + 1]
+                if t < PACK - by_vector:
+                    nc.scalar.activation(out=y_sb[:, t, :], in_=accs[t][:], func=IDENTITY, bias=b1_col, scale=1.0)
+                else:
+                    nc.vector.tensor_scalar_add(out=y_sb[:, t, :], in0=accs[t][:], scalar1=b1_col)
             return y_sb
 
-        def quantise_z(y_rect, y_plain, half):
-            cols = slice(half * N_TILE, (half + 1) * N_TILE)
-            z_plain = new_grouped()
-            regroup_on_scalar(z_plain[:], y_plain[:])
-            z_rect_in = new_grouped()
-            regroup_on_vector(z_rect_in[:], y_rect[:])
-            z_rect_out = new_grouped()
-            nc.vector.tensor_scalar_max(out=z_rect_out[:], in0=z_rect_in[:], scalar1=0.0)
-            quantise(z_rect_in, z_codes[:, 1, cols], z_scales[:, 1, cols])
-            quantise(z_rect_out, z_codes[:, 2, cols], z_scales[:, 2, cols])
-            quantise(z_plain, z_codes[:, 0, cols], z_scales[:, 0, cols])
-
         with tc.tile_pool(name="raw1", bufs=1) as raw1:
-            ident = keep.tile([P, P], BF16)
-            make_identity(nc, ident[:])
             bias_rows = keep.tile([P, P], BF16)
             nc.vector.memset(bias_rows[:], 0.0)
-            nc.sync.dma_start(out=bias_rows[0:M_TILES_1, :], in_=b1.rearrange("(m p) -> m p", p=P))
-            nc.sync.dma_start(
-                out=bias_rows[M_TILES_1 : M_TILES_1 + M_TILES_2, :], in_=b2.rearrange("(m p) -> m p", p=P)
-            )
+
+            w1_sides = []
+            x_raw = [[], []]
+
+            def load_x(half, g):
+                x_rows = raw1.tile([P, 2, PACK, PIXELS], BF16, name="x_raw%d_%d" % (half, g))
+                nc.sync.dma_start(
+                    out=x_rows[:],
+                    in_=x[2 * half : 2 * half + 2, g * K_PASS : (g + 1) * K_PASS].rearrange(
+                        "b (p j) r c -> p b j (r c)", j=PACK
+                    ),
+                )
+                x_raw[half].append(x_rows)
+
+            for g in range(PASSES_1):
+                load_x(0, g)
+                w1_rows = w1[g * K_PASS : (g + 1) * K_PASS, :].rearrange("(p j) d -> p j d", j=PACK)
+                if g == 0:
+                    w_rect = raw1.tile([P, PACK, BLOCK], BF16, name="w1_raw_rect")
+                    nc.sync.dma_start(out=w_rect[:], in_=w1_rows[:, :, BLOCK : 2 * BLOCK])
+                    w_plain = raw1.tile([P, PACK, BLOCK], BF16, name="w1_raw_plain")
+                    nc.sync.dma_start(out=w_plain[:], in_=w1_rows[:, :, 0:BLOCK])
+                    w1_sides.append((w_plain[:], w_rect[:]))
+                    nc.sync.dma_start(out=bias_rows[0:M_TILES_1, :], in_=b1.rearrange("(m p) -> m p", p=P))
+                    nc.sync.dma_start(
+                        out=bias_rows[M_TILES_1 : M_TILES_1 + M_TILES_2, :], in_=b2.rearrange("(m p) -> m p", p=P)
+                    )
+                else:
+                    w_rows = raw1.tile([P, PACK, HIDDEN], BF16, name="w1_raw%d" % g)
+                    nc.sync.dma_start(out=w_rows[:], in_=w1_rows)
+                    w1_sides.append((w_rows[:, :, 0:BLOCK], w_rows[:, :, BLOCK : 2 * BLOCK]))
+            for g in range(PASSES_1):
+                load_x(1, g)
+
+            ident = keep.tile([P, P], BF16)
+            make_identity(nc, ident[:])
             bias_ps = psum.tile([P, P], BF16, tag="acc")
             nc.tensor.transpose(bias_ps[:], bias_rows[:], ident[:])
             bias = keep.tile([P, M_TILES_1 + M_TILES_2], F32)
-            nc.vector.tensor_copy(out=bias[:], in_=bias_ps[:, 0 : M_TILES_1 + M_TILES_2])
 
-            w1_raw = []
-            x_raw = [[], []]
-            for half in range(HALVES):
-                for g in range(PASSES_1):
-                    k_rows = slice(g * K_PASS, (g + 1) * K_PASS)
-                    if half == 0:
-                        w_rows = raw1.tile([P, PACK, HIDDEN], BF16, name="w1_raw%d" % g)
-                        nc.sync.dma_start(out=w_rows[:], in_=w1[k_rows, :].rearrange("(p j) d -> p j d", j=PACK))
-                        w1_raw.append(w_rows)
-                    x_rows = raw1.tile([P, 2, PACK, PIXELS], BF16, name="x_raw%d_%d" % (half, g))
-                    nc.sync.dma_start(
-                        out=x_rows[:],
-                        in_=x[2 * half : 2 * half + 2, k_rows].rearrange("b (p j) r c -> p b j (r c)", j=PACK),
-                    )
-                    x_raw[half].append(x_rows)
-
-            def regroup_images(x_rows, scalar_helps):
+            def regroup_images(x_rows, vector_cols):
                 grouped = new_grouped()
-                regroup_on_vector(grouped[:, 0:PIXELS, :], x_rows[:, 0])
-                if scalar_helps:
-                    regroup_on_scalar(grouped[:, PIXELS : 2 * PIXELS, :], x_rows[:, 1])
-                else:
-                    regroup_on_vector(grouped[:, PIXELS : 2 * PIXELS, :], x_rows[:, 1])
+                for image in (0, 1):
+                    first = image * PIXELS
+                    cut = min(max(vector_cols - first, 0), PIXELS)
+                    if cut > 0:
+                        regroup_on_vector(grouped[:, first : first + cut, :], x_rows[:, image, :, 0:cut])
+                    if cut < PIXELS:
+                        regroup_on_scalar(grouped[:, first + cut : first + PIXELS, :], x_rows[:, image, :, cut:PIXELS])
                 return grouped
+
+            def quantise_w1(grouped, g, group):
+                cols = slice(group * BLOCK, (group + 1) * BLOCK)
+                quantise(grouped, w1_codes[:, g, cols], w1_scales[:, g, cols])
+
+            def quantise_x(grouped, g, half):
+                cols = slice(half * N_TILE, (half + 1) * N_TILE)
+                quantise(grouped, x_codes[:, g, cols], x_scales[:, g, cols])
+
+            def group_passes(accs, g, group, half):
+                for t in range(PACK):
+                    first_contraction_pass(accs[t], g, group * PACK + t, half)
 
             first_accs = {}
             for group in (RECTIFIED, PLAIN):
                 first_accs[group] = [new_bank() for t in range(PACK)]
-            for g in range(PASSES_1):
-                w_left = new_grouped()
-                regroup_on_vector(w_left[:], w1_raw[g][:, :, 0:BLOCK])
-                w_right = new_grouped()
-                regroup_on_scalar(w_right[:], w1_raw[g][:, :, BLOCK : 2 * BLOCK])
-                x_grouped = regroup_images(x_raw[0][g], True)
-                quantise(w_left, w1_codes[:, g, 0:BLOCK], w1_scales[:, g, 0:BLOCK])
-                quantise(w_right, w1_codes[:, g, BLOCK : 2 * BLOCK], w1_scales[:, g, BLOCK : 2 * BLOCK])
-                quantise(x_grouped, x_codes[:, g, 0:N_TILE], x_scales[:, g, 0:N_TILE])
-                for group in (RECTIFIED, PLAIN):
-                    for t in range(PACK):
-                        first_contraction_pass(first_accs[group][t], g, group * PACK + t, 0)
+            plain_ready = None
+            for g in range(PASSES_1 + 1):
+                if g < PASSES_1:
+                    x_grouped = regroup_images(x_raw[0][g], 256)
+                if g > 0:
+                    quantise_w1(plain_ready, g - 1, PLAIN)
+                    group_passes(first_accs[PLAIN], g - 1, PLAIN, 0)
+                if g < PASSES_1:
+                    rect_ready = regroup(w1_sides[g][RECTIFIED], RECT_V)
+                    plain_ready = regroup(w1_sides[g][PLAIN], LAST_V if g == PASSES_1 - 1 else 0)
+                    quantise_x(x_grouped, g, 0)
+                    quantise_w1(rect_ready, g, RECTIFIED)
+                    group_passes(first_accs[RECTIFIED], g, RECTIFIED, 0)
 
-            for first_g in range(0, PASSES_1, 2):
-                pair = [regroup_images(x_raw[1][g], first_g == 0) for g in (first_g, first_g + 1)]
-                for g, x_grouped in zip((first_g, first_g + 1), pair):
-                    quantise(x_grouped, x_codes[:, g, N_TILE:COLS], x_scales[:, g, N_TILE:COLS])
-                if first_g == 0:
-                    y_rect = empty_banks(first_accs[RECTIFIED], RECTIFIED)
-                    y_plain = empty_banks(first_accs[PLAIN], PLAIN)
+            nc.vector.tensor_copy(out=bias[:], in_=bias_ps[:, 0 : M_TILES_1 + M_TILES_2])
+
+            x_grouped = [regroup_images(x_raw[1][g], X1_V[g]) for g in (0, 1)]
+            y_rect = empty_banks(first_accs[RECTIFIED], RECTIFIED, EV[0])
+            quantise_x(x_grouped[0], 0, 1)
+            quantise_x(x_grouped[1], 1, 1)
+            x_grouped += [regroup_images(x_raw[1][g], X1_V[g]) for g in (2, 3)]
+            y_plain = empty_banks(first_accs[PLAIN], PLAIN, EV[1])
+            quantise_x(x_grouped[2], 2, 1)
+            quantise_x(x_grouped[3], 3, 1)
+
+            second_accs = {}
+            for group in (RECTIFIED, PLAIN):
+                second_accs[group] = [new_bank() for t in range(PACK)]
+                for g in range(PASSES_1):
+                    group_passes(second_accs[group], g, group, 1)
 
         with tc.tile_pool(name="raw2", bufs=1, reuse_waits="tile") as raw2:
             w2_raw = []
@@ -185,58 +235,85 @@ def tile_offm_pa_kernel(tc, x, w1, b1, w2, b2, out):
                     )
                     w2_raw.append(w_rows)
 
-            def quantise_w2(c):
-                cols = slice(c * BLOCK, (c + 1) * BLOCK)
-                grouped = []
-                for g in range(PASSES_2):
-                    w_rows = w2_raw[c * PASSES_2 + g]
-                    w_grouped = new_grouped()
-                    regroup_on_vector(w_grouped[:, 0:W2_VECTOR_COLS, :], w_rows[:, :, 0:W2_VECTOR_COLS])
-                    regroup_on_scalar(w_grouped[:, W2_VECTOR_COLS:BLOCK, :], w_rows[:, :, W2_VECTOR_COLS:BLOCK])
-                    grouped.append(w_grouped)
-                for g in range(PASSES_2):
-                    quantise(grouped[g], w2_codes[:, g, cols], w2_scales[:, g, cols])
+            def regroup_w2(c, g, first, width, vector_cols):
+                return regroup(w2_raw[c * PASSES_2 + g][:, :, first : first + width], vector_cols)
 
-            def second_contraction(c):
-                for half in range(HALVES):
-                    n_cols = slice(half * N_TILE, (half + 1) * N_TILE)
-                    for m in range(c * BLOCK // P, (c + 1) * BLOCK // P):
-                        acc = new_bank()
-                        for g in range(PASSES_2):
-                            nc.tensor.matmul_mx(
-                                out=acc[:],
-                                lhsT=w2_codes[:, g, m * P : (m + 1) * P].bitcast(FP8X4),
-                                lhsT_scale=w2_scales[:, g, m * P : (m + 1) * P],
-                                rhs=z_codes[:, g, n_cols].bitcast(FP8X4),
-                                rhs_scale=z_scales[:, g, n_cols],
-                                start=(g == 0),
-                                stop=(g == PASSES_2 - 1),
-                            )
-                        o_sb = o_pool.tile([P, N_TILE], F32, name="o_sb", tag="o_sb")
-                        b2_col = bias[:, M_TILES_1 + m : M_TILES_1 + m + 1]
-                        if m % PACK != PACK - 1:
-                            nc.scalar.activation(out=o_sb[:], in_=acc[:], func=IDENTITY, bias=b2_col, scale=1.0)
-                        else:
-                            nc.vector.tensor_scalar_add(out=o_sb[:], in0=acc[:], scalar1=b2_col)
-                        nc.sync.dma_start(
-                            out=out[2 * half : 2 * half + 2, m * P : (m + 1) * P].rearrange("b e r c -> e b (r c)"),
-                            in_=o_sb[:].rearrange("p (b w) -> p b w", b=2),
-                        )
+            def quantise_w2(grouped, c, g, first, width):
+                cols = slice(c * BLOCK + first, c * BLOCK + first + width)
+                quantise(grouped, w2_codes[:, g, cols], w2_scales[:, g, cols])
 
-            second_accs = {}
-            for group in (RECTIFIED, PLAIN):
-                second_accs[group] = [new_bank() for t in range(PACK)]
-                for g in range(PASSES_1):
-                    for t in range(PACK):
-                        first_contraction_pass(second_accs[group][t], g, group * PACK + t, 1)
+            def z_cols(g, half):
+                cols = slice(half * N_TILE, (half + 1) * N_TILE)
+                return z_codes[:, g, cols], z_scales[:, g, cols]
 
-            quantise_z(y_rect, y_plain, 0)
-            quantise_w2(0)
-            y_rect = empty_banks(second_accs[RECTIFIED], RECTIFIED)
-            y_plain = empty_banks(second_accs[PLAIN], PLAIN)
-            quantise_z(y_rect, y_plain, 1)
+            def second_contraction(m, half):
+                acc = new_bank()
+                n_cols = slice(half * N_TILE, (half + 1) * N_TILE)
+                order = (1, 2, 0)
+                for g in order:
+                    nc.tensor.matmul_mx(
+                        out=acc[:],
+                        lhsT=w2_codes[:, g, m * P : (m + 1) * P].bitcast(FP8X4),
+                        lhsT_scale=w2_scales[:, g, m * P : (m + 1) * P],
+                        rhs=z_codes[:, g, n_cols].bitcast(FP8X4),
+                        rhs_scale=z_scales[:, g, n_cols],
+                        start=(g == order[0]),
+                        stop=(g == order[-1]),
+                    )
+                return acc, m, half
 
+            def empty_output(acc, m, half):
+                o_sb = o_pool.tile([P, N_TILE], F32, name="o_sb", tag="o_sb")
+                b2_col = bias[:, M_TILES_1 + m : M_TILES_1 + m + 1]
+                if m % PACK != PACK - 1:
+                    nc.scalar.activation(out=o_sb[:], in_=acc[:], func=IDENTITY, bias=b2_col, scale=1.0)
+                else:
+                    nc.vector.tensor_scalar_add(out=o_sb[:], in0=acc[:], scalar1=b2_col)
+                nc.sync.dma_start(
+                    out=out[2 * half : 2 * half + 2, m * P : (m + 1) * P].rearrange("b e r c -> e b (r c)"),
+                    in_=o_sb[:].rearrange("p (b w) -> p b w", b=2),
+                )
+
+            HALF = BLOCK // 2
+
+            def z_rectified(y_rect, half):
+                z_in = regroup(y_rect[:], BLOCK)
+                z_out = new_grouped()
+                nc.vector.tensor_scalar_max(out=z_out[:], in0=z_in[:], scalar1=0.0)
+                return z_in, z_out
+
+            def quantise_z(y_rect, y_plain, half, vector_cols):
+                z_plain = regroup(y_plain[:], vector_cols)
+                z_in, z_out = z_rectified(y_rect, half)
+                quantise(z_in, *z_cols(1, half))
+                quantise(z_out, *z_cols(2, half))
+                quantise(z_plain, *z_cols(0, half))
+
+            quantise_z(y_rect, y_plain, 0, ZP_V[0])
+            if EARLY:
+                y_rect = empty_banks(second_accs[RECTIFIED], RECTIFIED, EV[2])
+            for first in range(0, BLOCK, W20):
+                grouped = [regroup_w2(0, g, first, W20, W20 * W2A_V // 512) for g in (1, 2, 0)]
+                for w_grouped, g in zip(grouped, (1, 2, 0)):
+                    quantise_w2(w_grouped, 0, g, first, W20)
+            if not EARLY:
+                y_rect = empty_banks(second_accs[RECTIFIED], RECTIFIED, EV[2])
+            y_plain = empty_banks(second_accs[PLAIN], PLAIN, EV[3])
+            quantise_z(y_rect, y_plain, 1, ZP_V[1])
+
+            full = []
+            waiting = []
             for c in range(W2_BLOCKS):
-                if c + 1 < W2_BLOCKS:
-                    quantise_w2(c + 1)
-                second_contraction(c)
+                for i in range(HALVES * PACK):
+                    full.append(second_contraction(c * PACK + i % PACK, i // PACK))
+                    if c + 1 < W2_BLOCKS:
+                        for j in SCHED[c].get(i, ()):
+                            g = (1, 2, 0)[j // 2]
+                            if j % 2 == 0:
+                                waiting.append(regroup_w2(c + 1, g, 0, BLOCK, W2_V[c]))
+                            else:
+                                quantise_w2(waiting.pop(0), c + 1, g, 0, BLOCK)
+                    while len(full) > (LAG if c < 3 else LAG3):
+                        empty_output(*full.pop(0))
+            for tile in full:
+                empty_output(*tile)

@@ -28,17 +28,17 @@ BLOCK = 512
 W2_BLOCKS = C_OUT // BLOCK
 W2_VECTOR_COLS = 320
 RECT_V = 512
-LAST_V = 192
-X1_V = (256, 256, 512, 384)
-EV = (0, 0, 0, 1)
+LAST_V = 128
+X1_V = (256, 256, 512, 512)
+EV = (0, 0, 0, 0)
 ZP_V = (0, 0)
 W2A_V = 320
 W20 = 512
 EARLY = 0
-LAG = 2
-LAG3 = 2
-W2_V = (320, 320, 384)
-SCHED = ({0: (0, 2, 1, 4, 3, 5)}, {0: (0,), 1: (2, 1), 2: (4, 3), 3: (5,)}, {0: (0,), 1: (2, 1), 2: (4, 3), 3: (5,)})
+LAG = 1
+LAG3 = 1
+W2_V = (320, 384, 320)
+SCHED = ({0: (0, 2, 1, 4, 3, 5)}, {0: (0, 2), 1: (1, 4), 2: (3, 5)}, {1: (0,), 2: (2, 1), 3: (4, 3), 4: (5,)})
 RUN = 8
 PLAIN, RECTIFIED = 0, 1
 
@@ -203,9 +203,9 @@ def tile_offm_pa_kernel(tc, x, w1, b1, w2, b2, out):
                     plain_ready = regroup(w1_sides[g][PLAIN], LAST_V if g == PASSES_1 - 1 else 0)
                     quantise_x(x_grouped, g, 0)
                     quantise_w1(rect_ready, g, RECTIFIED)
+                    if g == 0:
+                        nc.vector.tensor_copy(out=bias[:], in_=bias_ps[:, 0 : M_TILES_1 + M_TILES_2])
                     group_passes(first_accs[RECTIFIED], g, RECTIFIED, 0)
-
-            nc.vector.tensor_copy(out=bias[:], in_=bias_ps[:, 0 : M_TILES_1 + M_TILES_2])
 
             x_grouped = [regroup_images(x_raw[1][g], X1_V[g]) for g in (0, 1)]
             y_rect = empty_banks(first_accs[RECTIFIED], RECTIFIED, EV[0])
@@ -246,13 +246,13 @@ def tile_offm_pa_kernel(tc, x, w1, b1, w2, b2, out):
                 cols = slice(half * N_TILE, (half + 1) * N_TILE)
                 return z_codes[:, g, cols], z_scales[:, g, cols]
 
-            def second_contraction(m, half):
+            def second_contraction(m, n_first, width):
                 acc = new_bank()
-                n_cols = slice(half * N_TILE, (half + 1) * N_TILE)
+                n_cols = slice(n_first, n_first + width)
                 order = (1, 2, 0)
                 for g in order:
                     nc.tensor.matmul_mx(
-                        out=acc[:],
+                        out=acc[:, 0:width],
                         lhsT=w2_codes[:, g, m * P : (m + 1) * P].bitcast(FP8X4),
                         lhsT_scale=w2_scales[:, g, m * P : (m + 1) * P],
                         rhs=z_codes[:, g, n_cols].bitcast(FP8X4),
@@ -260,18 +260,20 @@ def tile_offm_pa_kernel(tc, x, w1, b1, w2, b2, out):
                         start=(g == order[0]),
                         stop=(g == order[-1]),
                     )
-                return acc, m, half
+                return acc, m, n_first, width
 
-            def empty_output(acc, m, half):
+            def empty_output(acc, m, n_first, width):
                 o_sb = o_pool.tile([P, N_TILE], F32, name="o_sb", tag="o_sb")
                 b2_col = bias[:, M_TILES_1 + m : M_TILES_1 + m + 1]
-                if m % PACK != PACK - 1:
-                    nc.scalar.activation(out=o_sb[:], in_=acc[:], func=IDENTITY, bias=b2_col, scale=1.0)
+                by_scalar = m % PACK != PACK - 1 or (width < N_TILE and n_first + width < COLS)
+                if by_scalar:
+                    nc.scalar.activation(out=o_sb[:, 0:width], in_=acc[:, 0:width], func=IDENTITY, bias=b2_col, scale=1.0)
                 else:
-                    nc.vector.tensor_scalar_add(out=o_sb[:], in0=acc[:], scalar1=b2_col)
+                    nc.vector.tensor_scalar_add(out=o_sb[:, 0:width], in0=acc[:, 0:width], scalar1=b2_col)
+                images = slice(n_first // PIXELS, (n_first + width) // PIXELS)
                 nc.sync.dma_start(
-                    out=out[2 * half : 2 * half + 2, m * P : (m + 1) * P].rearrange("b e r c -> e b (r c)"),
-                    in_=o_sb[:].rearrange("p (b w) -> p b w", b=2),
+                    out=out[images, m * P : (m + 1) * P].rearrange("b e r c -> e b (r c)"),
+                    in_=o_sb[:, 0:width].rearrange("p (b w) -> p b w", w=PIXELS),
                 )
 
             HALF = BLOCK // 2
@@ -305,7 +307,12 @@ def tile_offm_pa_kernel(tc, x, w1, b1, w2, b2, out):
             waiting = []
             for c in range(W2_BLOCKS):
                 for i in range(HALVES * PACK):
-                    full.append(second_contraction(c * PACK + i % PACK, i // PACK))
+                    m, n_first = c * PACK + i % PACK, i // PACK * N_TILE
+                    if m == M_TILES_2 - 1 and n_first > 0:
+                        full.append(second_contraction(m, n_first, PIXELS))
+                        full.append(second_contraction(m, n_first + PIXELS, PIXELS))
+                    else:
+                        full.append(second_contraction(m, n_first, N_TILE))
                     if c + 1 < W2_BLOCKS:
                         for j in SCHED[c].get(i, ()):
                             g = (1, 2, 0)[j // 2]

@@ -50,9 +50,9 @@ def tile_offm_pa_kernel(tc, x, w1, b1, w2, b2, out):
     with ExitStack() as ctx:
         ctx.enter_context(tc.manual_schedule())
         keep = ctx.enter_context(tc.tile_pool(name="keep", bufs=1))
-        grouped_pool = ctx.enter_context(tc.tile_pool(name="grouped", bufs=8))
-        y_pool = ctx.enter_context(tc.tile_pool(name="y", bufs=2))
-        o_pool = ctx.enter_context(tc.tile_pool(name="o", bufs=6))
+        grouped_pool = ctx.enter_context(tc.tile_pool(name="grouped", bufs=10))
+        y_pool = ctx.enter_context(tc.tile_pool(name="y", bufs=3))
+        o_pool = ctx.enter_context(tc.tile_pool(name="o", bufs=12))
         psum = ctx.enter_context(tc.psum_pool(name="psum", bufs=8))
 
         w1_codes = keep.tile([P, PASSES_1, HIDDEN], U32, align_bytes=64)

@@ -55,14 +55,14 @@ def tile_offm_pa_kernel(tc, x, w1, b1, w2, b2, out):
         o_pool = ctx.enter_context(tc.tile_pool(name="o", bufs=12))
         psum = ctx.enter_context(tc.psum_pool(name="psum", bufs=8))
 
-        w1_codes = keep.tile([P, PASSES_1, HIDDEN], U32, align_bytes=64)
-        w1_scales = keep.tile([P, PASSES_1, HIDDEN], U8, align_bytes=64)
-        x_codes = keep.tile([P, PASSES_1, COLS], U32, align_bytes=64)
-        x_scales = keep.tile([P, PASSES_1, COLS], U8, align_bytes=64)
-        z_codes = keep.tile([P, PASSES_2, COLS], U32, align_bytes=64)
-        z_scales = keep.tile([P, PASSES_2, COLS], U8, align_bytes=64)
-        w2_codes = keep.tile([P, PASSES_2, C_OUT], U32, align_bytes=64)
-        w2_scales = keep.tile([P, PASSES_2, C_OUT], U8, align_bytes=64)
+        w1_codes = keep.tile([P, PASSES_1, HIDDEN], U32, align_bytes=256)
+        w1_scales = keep.tile([P, PASSES_1, HIDDEN], U8, align_bytes=256)
+        x_codes = keep.tile([P, PASSES_1, COLS], U32, align_bytes=256)
+        x_scales = keep.tile([P, PASSES_1, COLS], U8, align_bytes=256)
+        z_codes = keep.tile([P, PASSES_2, COLS], U32, align_bytes=256)
+        z_scales = keep.tile([P, PASSES_2, COLS], U8, align_bytes=256)
+        w2_codes = keep.tile([P, PASSES_2, C_OUT], U32, align_bytes=256)
+        w2_scales = keep.tile([P, PASSES_2, C_OUT], U8, align_bytes=256)
 
         def regroup_views(grouped_cols, rows):
             return (

@@ -27,15 +27,17 @@ M_TILES_2 = C_OUT // P
 BLOCK = 512
 W2_BLOCKS = C_OUT // BLOCK
 W2_VECTOR_COLS = 320
-RECT_V = 512
+RECT_V = 448
 LAST_V = 128
 X1_V = (256, 256, 512, 512)
 EV = (0, 0, 0, 0)
 ZP_V = (0, 0)
-W2A_V = 320
+W2A_V = 384
 W20 = 512
 EARLY = 0
 LAG = 1
+PF = 0
+SPLIT_X0 = 1
 LAG3 = 1
 W2_V = (320, 384, 320)
 SCHED = ({0: (0, 2, 1, 4, 3, 5)}, {0: (0, 2), 1: (1, 4), 2: (3, 5)}, {1: (0,), 2: (2, 1), 3: (4, 3), 4: (5,)})
@@ -50,8 +52,8 @@ def tile_offm_pa_kernel(tc, x, w1, b1, w2, b2, out):
     with ExitStack() as ctx:
         ctx.enter_context(tc.manual_schedule())
         keep = ctx.enter_context(tc.tile_pool(name="keep", bufs=1))
-        grouped_pool = ctx.enter_context(tc.tile_pool(name="grouped", bufs=10))
-        y_pool = ctx.enter_context(tc.tile_pool(name="y", bufs=3))
+        grouped_pool = ctx.enter_context(tc.tile_pool(name="grouped", bufs=11))
+        y_pool = ctx.enter_context(tc.tile_pool(name="y", bufs=4))
         o_pool = ctx.enter_context(tc.tile_pool(name="o", bufs=12))
         psum = ctx.enter_context(tc.psum_pool(name="psum", bufs=8))
 
@@ -131,12 +133,14 @@ def tile_offm_pa_kernel(tc, x, w1, b1, w2, b2, out):
 
             def load_x(half, g):
                 x_rows = raw1.tile([P, 2, PACK, PIXELS], BF16, name="x_raw%d_%d" % (half, g))
-                nc.sync.dma_start(
-                    out=x_rows[:],
-                    in_=x[2 * half : 2 * half + 2, g * K_PASS : (g + 1) * K_PASS].rearrange(
-                        "b (p j) r c -> p b j (r c)", j=PACK
-                    ),
-                )
+                k_rows = slice(g * K_PASS, (g + 1) * K_PASS)
+                pieces = 2 if half == 0 and g < SPLIT_X0 else 1
+                for i in range(pieces):
+                    images = slice(2 // pieces * i, 2 // pieces * (i + 1))
+                    nc.sync.dma_start(
+                        out=x_rows[:, images],
+                        in_=x[2 * half : 2 * half + 2, k_rows][images].rearrange("b (p j) r c -> p b j (r c)", j=PACK),
+                    )
                 x_raw[half].append(x_rows)
 
             for g in range(PASSES_1):
@@ -249,7 +253,7 @@ def tile_offm_pa_kernel(tc, x, w1, b1, w2, b2, out):
             def second_contraction(m, n_first, width):
                 acc = new_bank()
                 n_cols = slice(n_first, n_first + width)
-                order = (1, 2, 0)
+                order = (0, 1, 2) if PF and n_first < N_TILE else (1, 2, 0)
                 for g in order:
                     nc.tensor.matmul_mx(
                         out=acc[:, 0:width],
@@ -276,20 +280,18 @@ def tile_offm_pa_kernel(tc, x, w1, b1, w2, b2, out):
                     in_=o_sb[:, 0:width].rearrange("p (b w) -> p b w", w=PIXELS),
                 )
 
-            HALF = BLOCK // 2
-
-            def z_rectified(y_rect, half):
+            def quantise_z(y_rect, y_plain, half, vector_cols):
+                plain_first = PF and half == 0
+                z_plain = regroup(y_plain[:], vector_cols)
                 z_in = regroup(y_rect[:], BLOCK)
                 z_out = new_grouped()
+                if plain_first:
+                    quantise(z_plain, *z_cols(0, half))
                 nc.vector.tensor_scalar_max(out=z_out[:], in0=z_in[:], scalar1=0.0)
-                return z_in, z_out
-
-            def quantise_z(y_rect, y_plain, half, vector_cols):
-                z_plain = regroup(y_plain[:], vector_cols)
-                z_in, z_out = z_rectified(y_rect, half)
                 quantise(z_in, *z_cols(1, half))
                 quantise(z_out, *z_cols(2, half))
-                quantise(z_plain, *z_cols(0, half))
+                if not plain_first:
+                    quantise(z_plain, *z_cols(0, half))
 
             quantise_z(y_rect, y_plain, 0, ZP_V[0])
             if EARLY:

from contextlib import ExitStack

import concourse.mybir as mybir
from concourse.masks import make_identity

F32 = mybir.dt.float32
BF16 = mybir.dt.bfloat16
U32 = mybir.dt.uint32
U8 = mybir.dt.uint8
FP8X4 = mybir.dt.float8_e4m3fn_x4
IDENTITY = mybir.ActivationFunctionType.Identity

P = 128
PACK = 4
K_PASS = P * PACK

IMAGES, C_IN, HIDDEN, PIXELS = 4, 2048, 1024, 256
C_MID = HIDDEN + HIDDEN // 2
C_OUT = 2048
COLS = IMAGES * PIXELS
N_TILE = 512
HALVES = COLS // N_TILE
PASSES_1 = C_IN // K_PASS
PASSES_2 = C_MID // K_PASS
M_TILES_1 = HIDDEN // P
M_TILES_2 = C_OUT // P
BLOCK = 512
W2_BLOCKS = C_OUT // BLOCK
W2_VECTOR_COLS = 320
RECT_V = 448
LAST_V = 128
X1_V = (256, 256, 512, 512)
EV = (0, 0, 0, 0)
ZP_V = (0, 0)
W2A_V = 384
W20 = 512
EARLY = 0
LAG = 1
PF = 0
SPLIT_X0 = 1
LAG3 = 1
W2_V = (320, 384, 320)
SCHED = ({0: (0, 2, 1, 4, 3, 5)}, {0: (0, 2), 1: (1, 4), 2: (3, 5)}, {1: (0,), 2: (2, 1), 3: (4, 3), 4: (5,)})
RUN = 8
PLAIN, RECTIFIED = 0, 1

FLOPS = 2 * COLS * (C_IN * HIDDEN + C_MID * C_OUT)


def tile_offm_pa_kernel(tc, x, w1, b1, w2, b2, out):
    nc = tc.nc
    with ExitStack() as ctx:
        ctx.enter_context(tc.manual_schedule())
        keep = ctx.enter_context(tc.tile_pool(name="keep", bufs=1))
        grouped_pool = ctx.enter_context(tc.tile_pool(name="grouped", bufs=11))
        y_pool = ctx.enter_context(tc.tile_pool(name="y", bufs=4))
        o_pool = ctx.enter_context(tc.tile_pool(name="o", bufs=12))
        psum = ctx.enter_context(tc.psum_pool(name="psum", bufs=8))

        w1_codes = keep.tile([P, PASSES_1, HIDDEN], U32, align_bytes=256)
        w1_scales = keep.tile([P, PASSES_1, HIDDEN], U8, align_bytes=256)
        x_codes = keep.tile([P, PASSES_1, COLS], U32, align_bytes=256)
        x_scales = keep.tile([P, PASSES_1, COLS], U8, align_bytes=256)
        z_codes = keep.tile([P, PASSES_2, COLS], U32, align_bytes=256)
        z_scales = keep.tile([P, PASSES_2, COLS], U8, align_bytes=256)
        w2_codes = keep.tile([P, PASSES_2, C_OUT], U32, align_bytes=256)
        w2_scales = keep.tile([P, PASSES_2, C_OUT], U8, align_bytes=256)

        def regroup_views(grouped_cols, rows):
            return (
                grouped_cols.rearrange("p (c i) t -> p c t i", i=RUN),
                rows.rearrange("p t (c i) -> p c t i", i=RUN),
            )

        def regroup_on_vector(grouped_cols, rows):
            dst, src = regroup_views(grouped_cols, rows)
            nc.vector.tensor_copy(out=dst, in_=src)

        def regroup_on_scalar(grouped_cols, rows):
            dst, src = regroup_views(grouped_cols, rows)
            nc.scalar.copy(out=dst, in_=src)

        def regroup(rows, vector_cols):
            width = rows.shape[2]
            grouped = new_grouped()
            if vector_cols > 0:
                regroup_on_vector(grouped[:, 0:vector_cols, :], rows[:, :, 0:vector_cols])
            if vector_cols < width:
                regroup_on_scalar(grouped[:, vector_cols:width, :], rows[:, :, vector_cols:width])
            return grouped

        def new_grouped():
            return grouped_pool.tile([P, BLOCK, PACK], BF16, align_bytes=64, name="grouped", tag="grouped")

        def quantise(grouped, codes, scales):
            width = codes.shape[1]
            nc.vector.quantize_mx(
                out=codes.bitcast(FP8X4),
                scales=scales,
                in_=grouped[:, 0:width, :].rearrange("p w t -> p (w t)"),
            )

        def new_bank():
            return psum.tile([P, N_TILE], F32, name="acc", tag="acc")

        def first_contraction_pass(acc, g, m, half):
            nc.tensor.matmul_mx(
                out=acc[:],
                lhsT=w1_codes[:, g, m * P : (m + 1) * P].bitcast(FP8X4),
                lhsT_scale=w1_scales[:, g, m * P : (m + 1) * P],
                rhs=x_codes[:, g, half * N_TILE : (half + 1) * N_TILE].bitcast(FP8X4),
                rhs_scale=x_scales[:, g, half * N_TILE : (half + 1) * N_TILE],
                start=(g == 0),
                stop=(g == PASSES_1 - 1),
            )

        def empty_banks(accs, group, by_vector):
            y_sb = y_pool.tile([P, PACK, N_TILE], BF16, name="y_sb", tag="y_sb")
            for t in range(PACK):
                b1_col = bias[:, group * PACK + t : group * PACK + t + 1]
                if t < PACK - by_vector:
                    nc.scalar.activation(out=y_sb[:, t, :], in_=accs[t][:], func=IDENTITY, bias=b1_col, scale=1.0)
                else:
                    nc.vector.tensor_scalar_add(out=y_sb[:, t, :], in0=accs[t][:], scalar1=b1_col)
            return y_sb

        with tc.tile_pool(name="raw1", bufs=1) as raw1:
            bias_rows = keep.tile([P, P], BF16)
            nc.vector.memset(bias_rows[:], 0.0)

            w1_sides = []
            x_raw = [[], []]

            def load_x(half, g):
                x_rows = raw1.tile([P, 2, PACK, PIXELS], BF16, name="x_raw%d_%d" % (half, g))
                k_rows = slice(g * K_PASS, (g + 1) * K_PASS)
                pieces = 2 if half == 0 and g < SPLIT_X0 else 1
                for i in range(pieces):
                    images = slice(2 // pieces * i, 2 // pieces * (i + 1))
                    nc.sync.dma_start(
                        out=x_rows[:, images],
                        in_=x[2 * half : 2 * half + 2, k_rows][images].rearrange("b (p j) r c -> p b j (r c)", j=PACK),
                    )
                x_raw[half].append(x_rows)

            for g in range(PASSES_1):
                load_x(0, g)
                w1_rows = w1[g * K_PASS : (g + 1) * K_PASS, :].rearrange("(p j) d -> p j d", j=PACK)
                if g == 0:
                    w_rect = raw1.tile([P, PACK, BLOCK], BF16, name="w1_raw_rect")
                    nc.sync.dma_start(out=w_rect[:], in_=w1_rows[:, :, BLOCK : 2 * BLOCK])
                    w_plain = raw1.tile([P, PACK, BLOCK], BF16, name="w1_raw_plain")
                    nc.sync.dma_start(out=w_plain[:], in_=w1_rows[:, :, 0:BLOCK])
                    w1_sides.append((w_plain[:], w_rect[:]))
                    nc.sync.dma_start(out=bias_rows[0:M_TILES_1, :], in_=b1.rearrange("(m p) -> m p", p=P))
                    nc.sync.dma_start(
                        out=bias_rows[M_TILES_1 : M_TILES_1 + M_TILES_2, :], in_=b2.rearrange("(m p) -> m p", p=P)
                    )
                else:
                    w_rows = raw1.tile([P, PACK, HIDDEN], BF16, name="w1_raw%d" % g)
                    nc.sync.dma_start(out=w_rows[:], in_=w1_rows)
                    w1_sides.append((w_rows[:, :, 0:BLOCK], w_rows[:, :, BLOCK : 2 * BLOCK]))
            for g in range(PASSES_1):
                load_x(1, g)

            ident = keep.tile([P, P], BF16)
            make_identity(nc, ident[:])
            bias_ps = psum.tile([P, P], BF16, tag="acc")
            nc.tensor.transpose(bias_ps[:], bias_rows[:], ident[:])
            bias = keep.tile([P, M_TILES_1 + M_TILES_2], F32)

            def regroup_images(x_rows, vector_cols):
                grouped = new_grouped()
                for image in (0, 1):
                    first = image * PIXELS
                    cut = min(max(vector_cols - first, 0), PIXELS)
                    if cut > 0:
                        regroup_on_vector(grouped[:, first : first + cut, :], x_rows[:, image, :, 0:cut])
                    if cut < PIXELS:
                        regroup_on_scalar(grouped[:, first + cut : first + PIXELS, :], x_rows[:, image, :, cut:PIXELS])
                return grouped

            def quantise_w1(grouped, g, group):
                cols = slice(group * BLOCK, (group + 1) * BLOCK)
                quantise(grouped, w1_codes[:, g, cols], w1_scales[:, g, cols])

            def quantise_x(grouped, g, half):
                cols = slice(half * N_TILE, (half + 1) * N_TILE)
                quantise(grouped, x_codes[:, g, cols], x_scales[:, g, cols])

            def group_passes(accs, g, group, half):
                for t in range(PACK):
                    first_contraction_pass(accs[t], g, group * PACK + t, half)

            first_accs = {}
            for group in (RECTIFIED, PLAIN):
                first_accs[group] = [new_bank() for t in range(PACK)]
            plain_ready = None
            for g in range(PASSES_1 + 1):
                if g < PASSES_1:
                    x_grouped = regroup_images(x_raw[0][g], 256)
                if g > 0:
                    quantise_w1(plain_ready, g - 1, PLAIN)
                    group_passes(first_accs[PLAIN], g - 1, PLAIN, 0)
                if g < PASSES_1:
                    rect_ready = regroup(w1_sides[g][RECTIFIED], RECT_V)
                    plain_ready = regroup(w1_sides[g][PLAIN], LAST_V if g == PASSES_1 - 1 else 0)
                    quantise_x(x_grouped, g, 0)
                    quantise_w1(rect_ready, g, RECTIFIED)
                    if g == 0:
                        nc.vector.tensor_copy(out=bias[:], in_=bias_ps[:, 0 : M_TILES_1 + M_TILES_2])
                    group_passes(first_accs[RECTIFIED], g, RECTIFIED, 0)

            x_grouped = [regroup_images(x_raw[1][g], X1_V[g]) for g in (0, 1)]
            y_rect = empty_banks(first_accs[RECTIFIED], RECTIFIED, EV[0])
            quantise_x(x_grouped[0], 0, 1)
            quantise_x(x_grouped[1], 1, 1)
            x_grouped += [regroup_images(x_raw[1][g], X1_V[g]) for g in (2, 3)]
            y_plain = empty_banks(first_accs[PLAIN], PLAIN, EV[1])
            quantise_x(x_grouped[2], 2, 1)
            quantise_x(x_grouped[3], 3, 1)

            second_accs = {}
            for group in (RECTIFIED, PLAIN):
                second_accs[group] = [new_bank() for t in range(PACK)]
                for g in range(PASSES_1):
                    group_passes(second_accs[group], g, group, 1)

        with tc.tile_pool(name="raw2", bufs=1, reuse_waits="tile") as raw2:
            w2_raw = []
            for c in range(W2_BLOCKS):
                for g in range(PASSES_2):
                    w_rows = raw2.tile([P, PACK, BLOCK], BF16, name="w2_raw%d_%d" % (c, g))
                    nc.sync.dma_start(
                        out=w_rows[:],
                        in_=w2[g * K_PASS : (g + 1) * K_PASS, c * BLOCK : (c + 1) * BLOCK].rearrange(
                            "(t p) e -> p t e", p=P
                        ),
                    )
                    w2_raw.append(w_rows)

            def regroup_w2(c, g, first, width, vector_cols):
                return regroup(w2_raw[c * PASSES_2 + g][:, :, first : first + width], vector_cols)

            def quantise_w2(grouped, c, g, first, width):
                cols = slice(c * BLOCK + first, c * BLOCK + first + width)
                quantise(grouped, w2_codes[:, g, cols], w2_scales[:, g, cols])

            def z_cols(g, half):
                cols = slice(half * N_TILE, (half + 1) * N_TILE)
                return z_codes[:, g, cols], z_scales[:, g, cols]

            def second_contraction(m, n_first, width):
                acc = new_bank()
                n_cols = slice(n_first, n_first + width)
                order = (0, 1, 2) if PF and n_first < N_TILE else (1, 2, 0)
                for g in order:
                    nc.tensor.matmul_mx(
                        out=acc[:, 0:width],
                        lhsT=w2_codes[:, g, m * P : (m + 1) * P].bitcast(FP8X4),
                        lhsT_scale=w2_scales[:, g, m * P : (m + 1) * P],
                        rhs=z_codes[:, g, n_cols].bitcast(FP8X4),
                        rhs_scale=z_scales[:, g, n_cols],
                        start=(g == order[0]),
                        stop=(g == order[-1]),
                    )
                return acc, m, n_first, width

            def empty_output(acc, m, n_first, width):
                o_sb = o_pool.tile([P, N_TILE], F32, name="o_sb", tag="o_sb")
                b2_col = bias[:, M_TILES_1 + m : M_TILES_1 + m + 1]
                by_scalar = m % PACK != PACK - 1 or (width < N_TILE and n_first + width < COLS)
                if by_scalar:
                    nc.scalar.activation(out=o_sb[:, 0:width], in_=acc[:, 0:width], func=IDENTITY, bias=b2_col, scale=1.0)
                else:
                    nc.vector.tensor_scalar_add(out=o_sb[:, 0:width], in0=acc[:, 0:width], scalar1=b2_col)
                images = slice(n_first // PIXELS, (n_first + width) // PIXELS)
                nc.sync.dma_start(
                    out=out[images, m * P : (m + 1) * P].rearrange("b e r c -> e b (r c)"),
                    in_=o_sb[:, 0:width].rearrange("p (b w) -> p b w", w=PIXELS),
                )

            def quantise_z(y_rect, y_plain, half, vector_cols):
                plain_first = PF and half == 0
                z_plain = regroup(y_plain[:], vector_cols)
                z_in = regroup(y_rect[:], BLOCK)
                z_out = new_grouped()
                if plain_first:
                    quantise(z_plain, *z_cols(0, half))
                nc.vector.tensor_scalar_max(out=z_out[:], in0=z_in[:], scalar1=0.0)
                quantise(z_in, *z_cols(1, half))
                quantise(z_out, *z_cols(2, half))
                if not plain_first:
                    quantise(z_plain, *z_cols(0, half))

            quantise_z(y_rect, y_plain, 0, ZP_V[0])
            if EARLY:
                y_rect = empty_banks(second_accs[RECTIFIED], RECTIFIED, EV[2])
            for first in range(0, BLOCK, W20):
                grouped = [regroup_w2(0, g, first, W20, W20 * W2A_V // 512) for g in (1, 2, 0)]
                for w_grouped, g in zip(grouped, (1, 2, 0)):
                    quantise_w2(w_grouped, 0, g, first, W20)
            if not EARLY:
                y_rect = empty_banks(second_accs[RECTIFIED], RECTIFIED, EV[2])
            y_plain = empty_banks(second_accs[PLAIN], PLAIN, EV[3])
            quantise_z(y_rect, y_plain, 1, ZP_V[1])

            full = []
            waiting = []
            for c in range(W2_BLOCKS):
                for i in range(HALVES * PACK):
                    m, n_first = c * PACK + i % PACK, i // PACK * N_TILE
                    if m == M_TILES_2 - 1 and n_first > 0:
                        full.append(second_contraction(m, n_first, PIXELS))
                        full.append(second_contraction(m, n_first + PIXELS, PIXELS))
                    else:
                        full.append(second_contraction(m, n_first, N_TILE))
                    if c + 1 < W2_BLOCKS:
                        for j in SCHED[c].get(i, ()):
                            g = (1, 2, 0)[j // 2]
                            if j % 2 == 0:
                                waiting.append(regroup_w2(c + 1, g, 0, BLOCK, W2_V[c]))
                            else:
                                quantise_w2(waiting.pop(0), c + 1, g, 0, BLOCK)
                    while len(full) > (LAG if c < 3 else LAG3):
                        empty_output(*full.pop(0))
            for tile in full:
                empty_output(*tile)
